import numpy as np
import ml_dtypes


def mxq(x, axis, fmt="e4m3"):
    dtype, down = {"e4m3": (ml_dtypes.float8_e4m3fn, 7), "e5m2": (ml_dtypes.float8_e5m2, 14)}[fmt]
    v = np.moveaxis(np.asarray(x, np.float32).astype(ml_dtypes.bfloat16).astype(np.float64), axis, -1)
    blocks = v.reshape(v.shape[:-1] + (-1, 32))
    amax = np.abs(blocks).max(-1, keepdims=True)
    byte = np.maximum(np.where(amax > 0, np.frexp(amax)[1] - 1 + 127, 0) - down, 1)
    scale = np.exp2(byte - 127.0)
    codes = (blocks / scale).astype(np.float32).astype(dtype).astype(np.float64)
    return np.moveaxis((codes * scale).reshape(v.shape), -1, axis)


WIDE = False


def mx_kscale(k):
    if not WIDE:
        return np.ones(k)
    levels = np.array([10, -10, 5, -5, 0])
    a = np.random.permutation(np.resize(levels, k // 512 * 4)).reshape(k // 512, 4)
    idx = np.arange(k)
    return np.exp2(a[idx // 512, idx % 128 // 32])


BF16 = ml_dtypes.bfloat16


def bf(x):
    return np.asarray(x, np.float32).astype(BF16)


def f64(x):
    return np.asarray(x).astype(np.float64)


M, N, IN_CH, HID, N_CLS, DEG = 12288, 512, 512, 128, 40, 24


def setup_inputs():
    s = mx_kscale(IN_CH)
    return {"x": bf(np.random.standard_normal((N, IN_CH)) * s),
            "adj": bf(np.random.uniform(size=(M, N)) < DEG / N),
            "W_in": bf(np.random.standard_normal((IN_CH, HID)) * 2.0 / np.sqrt(IN_CH) / s[:, None]),
            "b_in": bf(np.random.standard_normal(HID) * 0.3)}


def reference(x, adj, W_in, b_in):
    a = f64(adj)
    h = (mxq(f64(x), 1, "e4m3") @ mxq(f64(W_in), 0, "e4m3")) + f64(b_in)
    deg = np.sum(a, axis=1, keepdims=True)
    return (mxq(a, 1, "e4m3") @ mxq(h, 0, "e4m3")) / (deg + 1.0)

@@ -1,0 +1,239 @@
+from contextlib import ExitStack
+
+import concourse.mybir as mybir
+from concourse.masks import make_identity
+
+F32 = mybir.dt.float32
+BF16 = mybir.dt.bfloat16
+U32 = mybir.dt.uint32
+U8 = mybir.dt.uint8
+FP8X4 = mybir.dt.float8_e4m3fn_x4
+ALU = mybir.AluOpType
+ACT = mybir.ActivationFunctionType
+
+P = 128
+FLOPS = 2 * 12288 * 512 * 128 + 2 * 512 * 512 * 128
+
+CHUNK_TILES = [4, 4] + [8] * 11
+GROUP = 4
+LAG_MX = 3
+S_DEG = {1: 2, 2: 2, 4: 1, 6: 1, 8: 1, 10: 1, 12: 1, 14: 1, 16: 1, 18: 1}
+V_OUT = (22, 23)
+
+
+def tile_allgnn_pa_t_kernel(tc, x, adj, W_in, b_in, out):
+    nc = tc.nc
+    n_groups = sum(CHUNK_TILES) // GROUP
+    with ExitStack() as ctx:
+        ctx.enter_context(tc.manual_schedule())
+        const = ctx.enter_context(tc.tile_pool(name="const", bufs=1))
+        gpool = ctx.enter_context(tc.tile_pool(name="grouped", bufs=3))
+        cpool = ctx.enter_context(tc.tile_pool(name="codes", bufs=5))
+        rpool = ctx.enter_context(tc.tile_pool(name="res", bufs=4))
+        jpool = ctx.enter_context(tc.tile_pool(name="junk", bufs=4))
+        tps = ctx.enter_context(tc.psum_pool(name="tps", bufs=4))
+        ops = ctx.enter_context(tc.psum_pool(name="ops", bufs=3))
+
+        ident = const.tile([P, P], F32)
+        make_identity(nc, ident[:])
+        ones = const.tile([P, P], BF16)
+        nc.vector.memset(ones[:], 1.0)
+        bz = const.tile([P, P], BF16)
+        nc.vector.memset(bz[:], 0.0)
+        nc.scalar.dma_start(out=bz[0:1, :], in_=b_in.unsqueeze(0))
+
+        adj_sb = []
+        out_dst = []
+        place = []
+        x_sb = const.tile([P, 4, 512], BF16)
+        w_sb = const.tile([P, 4, P], BF16)
+        row0 = 0
+        for ci, nt in enumerate(CHUNK_TILES):
+            a_t = const.tile([P, nt, 512], BF16, name="adj%d" % ci)
+            nc.sync.dma_start(
+                out=a_t[:], in_=adj[row0 : row0 + P * nt, :].rearrange("(p t) k -> p t k", t=nt)
+            )
+            adj_sb.append(a_t)
+            out_dst.append(out[row0 : row0 + P * nt, :].rearrange("(p t) c -> p t c", t=nt))
+            for t0 in range(0, nt, GROUP):
+                place.append((ci, t0))
+            row0 += P * nt
+            if ci == 0:
+                nc.sync.dma_start(
+                    out=x_sb[:].rearrange("p (u e) f -> p u e f", u=2),
+                    in_=x.rearrange("(u p e) f -> p u e f", u=2, p=P, e=2),
+                )
+                nc.sync.dma_start(
+                    out=w_sb[:].rearrange("p (u e) c -> p u e c", u=2),
+                    in_=W_in.rearrange("(u p e) c -> p u e c", u=2, p=P, e=2),
+                )
+
+        degp1 = const.tile([P, 96], F32)
+        recip = const.tile([P, 96], F32)
+        deg_s = const.tile([P, 96], F32)
+        bias_sb = const.tile([P, P], F32)
+        w_g = const.tile([P, P, 4], BF16, align_bytes=64)
+        w_codes = const.tile([P, P], U32, align_bytes=64)
+        w_scl = const.tile([P, P], U8, align_bytes=64)
+        x_g = const.tile([P, 4, P, 2], F32, align_bytes=64)
+        x_codes = const.tile([P, 4 * P], U32, align_bytes=64)
+        x_scl = const.tile([P, 4 * P], U8, align_bytes=64)
+        h_g = const.tile([P, P, 4], BF16, align_bytes=64)
+        h_codes = const.tile([P, P], U32, align_bytes=64)
+        h_scl = const.tile([P, P], U8, align_bytes=64)
+
+        banks = {}
+        grouped = {}
+        codes = {}
+        scales = {}
+        acc = {}
+
+        def word_transposes(key, rows_of):
+            pair = []
+            for half in range(2):
+                tp = tps.tile([P, 2, 2, P], F32, name="tp")
+                for a in range(2):
+                    words = rows_of(2 * half + a).bitcast(F32)
+                    for u in range(2):
+                        nc.tensor.transpose(tp[:, a, u, :], words[:, u * P : (u + 1) * P], ident[:])
+                pair.append(tp)
+            banks[key] = pair
+
+        def evacuate(key, dst):
+            for half in range(2):
+                nc.scalar.copy(
+                    out=dst[:, 2 * half : 2 * half + 2, :, :],
+                    in_=banks[key][half][:].rearrange("p a u m -> p a m u"),
+                )
+
+        def quantise(src_bf16, c_t, s_t):
+            nc.vector.quantize_mx(out=c_t[:].bitcast(FP8X4), scales=s_t[:], in_=src_bf16)
+
+        def adj_rows(g):
+            ci, t0 = place[g]
+            return lambda j: adj_sb[ci][:, t0 + j, :]
+
+        def degree(g, tiles):
+            rows_of = adj_rows(g)
+            n_s = S_DEG.get(g, 0)
+            for a in tiles:
+                col = GROUP * g + a
+                if a >= GROUP - n_s:
+                    junk_s = jpool.tile([P, 512], BF16, name="junk_s")
+                    nc.scalar.activation(
+                        out=junk_s[:], in_=rows_of(a), func=ACT.Copy, accum_out=deg_s[:, col : col + 1]
+                    )
+                else:
+                    junk_v = jpool.tile([P, 512], BF16, name="junk_v")
+                    nc.vector.tensor_scalar(
+                        out=junk_v[:],
+                        in0=rows_of(a),
+                        scalar1=1.0,
+                        scalar2=1.0,
+                        op0=ALU.mult,
+                        op1=ALU.add,
+                        accum_out=degp1[:, col : col + 1],
+                    )
+
+        def reciprocals(g):
+            n_s = S_DEG.get(g, 0)
+            lo = GROUP * g
+            if n_s:
+                nc.vector.tensor_scalar_add(
+                    out=degp1[:, lo + GROUP - n_s : lo + GROUP],
+                    in0=deg_s[:, lo + GROUP - n_s : lo + GROUP],
+                    scalar1=1.0,
+                )
+            nc.vector.reciprocal(out=recip[:, lo : lo + GROUP], in_=degp1[:, lo : lo + GROUP])
+
+        def multiply(g):
+            o_t = ops.tile([P, GROUP, P], F32, name="o_t")
+            for a in range(GROUP):
+                cols = slice(a * P, (a + 1) * P)
+                nc.tensor.matmul_mx(
+                    out=o_t[:, a, :],
+                    lhsT=codes[g][:, cols].bitcast(FP8X4),
+                    lhsT_scale=scales[g][:, cols],
+                    rhs=h_codes[:].bitcast(FP8X4),
+                    rhs_scale=h_scl[:],
+                    start=True,
+                    stop=True,
+                )
+            acc[g] = o_t
+
+        def finish(g):
+            ci, t0 = place[g]
+            lo = GROUP * g
+            res = rpool.tile([P, GROUP, P], F32, name="res")
+            if g in V_OUT:
+                nc.vector.tensor_tensor(
+                    out=res[:],
+                    in0=acc[g][:],
+                    in1=recip[:, lo : lo + GROUP].unsqueeze(2).to_broadcast([P, GROUP, P]),
+                    op=ALU.mult,
+                )
+            else:
+                for a in range(GROUP):
+                    nc.scalar.activation(
+                        out=res[:, a, :],
+                        in_=acc[g][:, a, :],
+                        func=ACT.Copy,
+                        scale=recip[:, lo + a : lo + a + 1],
+                    )
+            nc.sync.dma_start(out=out_dst[ci][:, t0 : t0 + GROUP, :], in_=res[:])
+
+        for i in range(n_groups + LAG_MX):
+            if i < n_groups:
+                word_transposes(i, adj_rows(i))
+                g_t = gpool.tile([P, GROUP, P, 2], F32, name="g_t", align_bytes=64)
+                grouped[i] = g_t
+                evacuate(i, g_t)
+            if i == 0:
+                b_ps = ops.tile([P, GROUP, P], F32, name="o_t")
+                nc.tensor.matmul(out=b_ps[:, 0, :], lhsT=ones[:], rhs=bz[:], start=True, stop=True)
+                nc.scalar.copy(out=bias_sb[:], in_=b_ps[:, 0, :])
+                word_transposes("x", lambda j: x_sb[:, j, :])
+                evacuate("x", x_g)
+                degree(0, range(GROUP))
+                nc.vector.tensor_copy(out=w_g[:], in_=w_sb[:].rearrange("p t c -> p c t"))
+                continue
+            if i - 1 < n_groups:
+                c_t = cpool.tile([P, GROUP * P], U32, name="c_t", align_bytes=64)
+                s_t = cpool.tile([P, GROUP * P], U8, name="s_t", align_bytes=64)
+                codes[i - 1] = c_t
+                scales[i - 1] = s_t
+                quantise(grouped[i - 1][:].rearrange("p a m u -> p (a m u)").bitcast(BF16), c_t, s_t)
+                if i == 1:
+                    quantise(w_g[:].rearrange("p c t -> p (c t)"), w_codes, w_scl)
+                reciprocals(i - 1)
+            if i == 2:
+                nc.vector.tensor_tensor(
+                    out=h_g[:],
+                    in0=acc["h"][:].rearrange("p t c -> p c t"),
+                    in1=bias_sb[:].unsqueeze(2).to_broadcast([P, P, 4]),
+                    op=ALU.add,
+                )
+            if i < n_groups:
+                degree(i, range(0, 2))
+            if i == 1:
+                quantise(x_g[:].rearrange("p a m u -> p (a m u)").bitcast(BF16), x_codes, x_scl)
+                h_ps = ops.tile([P, GROUP, P], F32, name="o_t")
+                for t in range(4):
+                    cols = slice(t * P, (t + 1) * P)
+                    nc.tensor.matmul_mx(
+                        out=h_ps[:, t, :],
+                        lhsT=x_codes[:, cols].bitcast(FP8X4),
+                        lhsT_scale=x_scl[:, cols],
+                        rhs=w_codes[:].bitcast(FP8X4),
+                        rhs_scale=w_scl[:],
+                        start=True,
+                        stop=True,
+                    )
+                acc["h"] = h_ps
+            if i == 2:
+                quantise(h_g[:].rearrange("p c t -> p (c t)"), h_codes, h_scl)
+            if i < n_groups:
+                degree(i, range(2, GROUP))
+            if i >= LAG_MX:
+                multiply(i - LAG_MX)
+                finish(i - LAG_MX)

@@ -27,11 +27,11 @@ def tile_allgnn_pa_t_kernel(tc, x, adj, W_in, b_in, out):
     with ExitStack() as ctx:
         ctx.enter_context(tc.manual_schedule())
         const = ctx.enter_context(tc.tile_pool(name="const", bufs=1))
-        gpool = ctx.enter_context(tc.tile_pool(name="grouped", bufs=3))
+        gpool = ctx.enter_context(tc.tile_pool(name="grouped", bufs=4))
         cpool = ctx.enter_context(tc.tile_pool(name="codes", bufs=5))
-        rpool = ctx.enter_context(tc.tile_pool(name="res", bufs=4))
+        rpool = ctx.enter_context(tc.tile_pool(name="res", bufs=24))
         jpool = ctx.enter_context(tc.tile_pool(name="junk", bufs=4))
-        tps = ctx.enter_context(tc.psum_pool(name="tps", bufs=4))
+        tps = ctx.enter_context(tc.psum_pool(name="tps", bufs=5))
         ops = ctx.enter_context(tc.psum_pool(name="ops", bufs=3))
 
         ident = const.tile([P, P], F32)

@@ -10,37 +10,88 @@ U8 = mybir.dt.uint8
 FP8X4 = mybir.dt.float8_e4m3fn_x4
 ALU = mybir.AluOpType
 ACT = mybir.ActivationFunctionType
+AX = mybir.AxisListType
 
 P = 128
 FLOPS = 2 * 12288 * 512 * 128 + 2 * 512 * 512 * 128
 
 CHUNK_TILES = [4, 4] + [8] * 11
 GROUP = 4
-LAG_MX = 3
-S_DEG = {1: 2, 2: 2, 4: 1, 6: 1, 8: 1, 10: 1, 12: 1, 14: 1, 16: 1, 18: 1}
-V_OUT = (22, 23)
+N_GROUPS = 24
+LAG = 6
+PE_BATCHES = ((0, 1, 2, 3), (12, 13, 14, 15))
+V_OUT = (5, 10, 15, 20, 22, 23)
+DEG_PER_ROUND = 3
+DEG_N = 32
+WARM = 3
+
+
+def degree_plan():
+    on_pe = [g for b in PE_BATCHES for g in b]
+    todo = [(g, a) for g in range(N_GROUPS) if g not in on_pe for a in range(GROUP)]
+    plan = []
+    k = 0
+    for i in range(N_GROUPS + LAG):
+        now = []
+        while len(now) < DEG_PER_ROUND and k < len(todo) and todo[k][0] <= i + i // 3:
+            now.append(todo[k])
+            k += 1
+        plan.append(now)
+    assert k == len(todo)
+    return plan
 
 
 def tile_allgnn_pa_t_kernel(tc, x, adj, W_in, b_in, out):
     nc = tc.nc
-    n_groups = sum(CHUNK_TILES) // GROUP
+    on_pe = [g for b in PE_BATCHES for g in b]
+    plan = degree_plan()
     with ExitStack() as ctx:
         ctx.enter_context(tc.manual_schedule())
         const = ctx.enter_context(tc.tile_pool(name="const", bufs=1))
         gpool = ctx.enter_context(tc.tile_pool(name="grouped", bufs=4))
-        cpool = ctx.enter_context(tc.tile_pool(name="codes", bufs=5))
-        rpool = ctx.enter_context(tc.tile_pool(name="res", bufs=24))
+        cpool = ctx.enter_context(tc.tile_pool(name="codes", bufs=LAG + 3))
+        rpool = ctx.enter_context(tc.tile_pool(name="res", bufs=N_GROUPS))
         jpool = ctx.enter_context(tc.tile_pool(name="junk", bufs=4))
-        tps = ctx.enter_context(tc.psum_pool(name="tps", bufs=5))
-        ops = ctx.enter_context(tc.psum_pool(name="ops", bufs=3))
+        tps = ctx.enter_context(tc.psum_pool(name="tps", bufs=4))
+        ops = ctx.enter_context(tc.psum_pool(name="ops", bufs=2))
+        dps = ctx.enter_context(tc.psum_pool(name="dps", bufs=1))
+
+        zc = const.tile([P, 512], U32, align_bytes=64)
+        zs = const.tile([P, 512], U8, align_bytes=64)
+        bz = const.tile([P, P], BF16)
+        nc.vector.memset(bz[:], 0.0)
+        nc.scalar.dma_start(out=bz[0:1, :], in_=b_in.unsqueeze(0))
+        zsrc = const.tile([P, 2048], BF16, align_bytes=64)
+        nc.vector.memset(zsrc[:], 0.0)
+        nc.vector.quantize_mx(out=zc[:].bitcast(FP8X4), scales=zs[:], in_=zsrc[:])
+        idle_ps = dps.tile([P, 512], F32, name="idle_ps")
+
+        def idle_pass():
+            nc.tensor.matmul_mx(
+                out=idle_ps[:],
+                lhsT=zc[:, 0:P].bitcast(FP8X4),
+                lhsT_scale=zs[:, 0:P],
+                rhs=zc[:].bitcast(FP8X4),
+                rhs_scale=zs[:],
+                start=True,
+                stop=True,
+            )
+
+        for w in range(WARM):
+            idle_pass()
 
         ident = const.tile([P, P], F32)
         make_identity(nc, ident[:])
         ones = const.tile([P, P], BF16)
         nc.vector.memset(ones[:], 1.0)
-        bz = const.tile([P, P], BF16)
-        nc.vector.memset(bz[:], 0.0)
-        nc.scalar.dma_start(out=bz[0:1, :], in_=b_in.unsqueeze(0))
+        quad = const.tile([P, 32], F32)
+        nc.vector.tensor_reduce(
+            out=quad[:], in_=ident[:].rearrange("p (m t) -> p m t", t=4), axis=AX.X, op=ALU.add
+        )
+        sel = const.tile([P, 4, P], F32)
+        nc.vector.memset(sel[:], 0.0)
+        for j in range(4):
+            nc.vector.tensor_copy(out=sel[:, j, 32 * j : 32 * j + 32], in_=quad[:])
 
         adj_sb = []
         out_dst = []
@@ -70,7 +121,6 @@ def tile_allgnn_pa_t_kernel(tc, x, adj, W_in, b_in, out):
 
         degp1 = const.tile([P, 96], F32)
         recip = const.tile([P, 96], F32)
-        deg_s = const.tile([P, 96], F32)
         bias_sb = const.tile([P, P], F32)
         w_g = const.tile([P, P, 4], BF16, align_bytes=64)
         w_codes = const.tile([P, P], U32, align_bytes=64)
@@ -81,12 +131,17 @@ def tile_allgnn_pa_t_kernel(tc, x, adj, W_in, b_in, out):
         h_g = const.tile([P, P, 4], BF16, align_bytes=64)
         h_codes = const.tile([P, P], U32, align_bytes=64)
         h_scl = const.tile([P, P], U8, align_bytes=64)
+        part = {}
+        for b in PE_BATCHES:
+            p_t = const.tile([P, 4, GROUP * len(b)], F32, name="part%d" % b[0])
+            part[b[0]] = p_t
 
         banks = {}
         grouped = {}
         codes = {}
         scales = {}
         acc = {}
+        fixed = {}
 
         def word_transposes(key, rows_of):
             pair = []
@@ -113,38 +168,51 @@ def tile_allgnn_pa_t_kernel(tc, x, adj, W_in, b_in, out):
             ci, t0 = place[g]
             return lambda j: adj_sb[ci][:, t0 + j, :]
 
-        def degree(g, tiles):
-            rows_of = adj_rows(g)
-            n_s = S_DEG.get(g, 0)
-            for a in tiles:
-                col = GROUP * g + a
-                if a >= GROUP - n_s:
-                    junk_s = jpool.tile([P, 512], BF16, name="junk_s")
-                    nc.scalar.activation(
-                        out=junk_s[:], in_=rows_of(a), func=ACT.Copy, accum_out=deg_s[:, col : col + 1]
-                    )
-                else:
-                    junk_v = jpool.tile([P, 512], BF16, name="junk_v")
-                    nc.vector.tensor_scalar(
-                        out=junk_v[:],
-                        in0=rows_of(a),
-                        scalar1=1.0,
-                        scalar2=1.0,
-                        op0=ALU.mult,
-                        op1=ALU.add,
-                        accum_out=degp1[:, col : col + 1],
-                    )
+        def flat_bf16(t4):
+            return t4[:].rearrange("p a m u -> p (a m u)").bitcast(BF16)
 
-        def reciprocals(g):
-            n_s = S_DEG.get(g, 0)
-            lo = GROUP * g
-            if n_s:
-                nc.vector.tensor_scalar_add(
-                    out=degp1[:, lo + GROUP - n_s : lo + GROUP],
-                    in0=deg_s[:, lo + GROUP - n_s : lo + GROUP],
-                    scalar1=1.0,
+        def degree_on_vector(g, a):
+            col = GROUP * g + a
+            junk_v = jpool.tile([P, 512], BF16, name="junk_v")
+            nc.vector.tensor_scalar(
+                out=junk_v[:],
+                in0=adj_rows(g)(a),
+                scalar1=1.0,
+                scalar2=1.0,
+                op0=ALU.mult,
+                op1=ALU.add,
+                accum_out=degp1[:, col : col + 1],
+            )
+
+        def partial_degrees(g, b):
+            d_t = dps.tile([P, 4 * GROUP, DEG_N], F32, name="d_t")
+            src = flat_bf16(grouped[g])
+            for s in range(4 * GROUP):
+                nc.tensor.matmul(
+                    out=d_t[:, s, :],
+                    lhsT=src[:, s * P : (s + 1) * P],
+                    rhs=ones[:, 0:DEG_N],
+                    start=True,
+                    stop=True,
                 )
-            nc.vector.reciprocal(out=recip[:, lo : lo + GROUP], in_=degp1[:, lo : lo + GROUP])
+            lo = GROUP * (g - b[0])
+            nc.scalar.copy(
+                out=part[b[0]][:, :, lo : lo + GROUP],
+                in_=d_t[:, :, 0].rearrange("p (a j) -> p j a", j=4),
+            )
+
+        def fold_degrees(b):
+            n = GROUP * len(b)
+            d_t = dps.tile([P, 4 * GROUP, DEG_N], F32, name="d_t")
+            for j in range(4):
+                nc.tensor.matmul(
+                    out=d_t[:, 0, 0:n],
+                    lhsT=sel[:, j, :],
+                    rhs=part[b[0]][:, j, :],
+                    start=(j == 0),
+                    stop=(j == 3),
+                )
+            fixed[b[0]] = d_t
 
         def multiply(g):
             o_t = ops.tile([P, GROUP, P], F32, name="o_t")
@@ -182,8 +250,11 @@ def tile_allgnn_pa_t_kernel(tc, x, adj, W_in, b_in, out):
                     )
             nc.sync.dma_start(out=out_dst[ci][:, t0 : t0 + GROUP, :], in_=res[:])
 
-        for i in range(n_groups + LAG_MX):
-            if i < n_groups:
+        summed = {}
+        waiting = []
+        for i in range(N_GROUPS + LAG):
+            busy = 0
+            if i < N_GROUPS:
                 word_transposes(i, adj_rows(i))
                 g_t = gpool.tile([P, GROUP, P, 2], F32, name="g_t", align_bytes=64)
                 grouped[i] = g_t
@@ -194,18 +265,32 @@ def tile_allgnn_pa_t_kernel(tc, x, adj, W_in, b_in, out):
                 nc.scalar.copy(out=bias_sb[:], in_=b_ps[:, 0, :])
                 word_transposes("x", lambda j: x_sb[:, j, :])
                 evacuate("x", x_g)
-                degree(0, range(GROUP))
                 nc.vector.tensor_copy(out=w_g[:], in_=w_sb[:].rearrange("p t c -> p c t"))
-                continue
-            if i - 1 < n_groups:
+            if 1 <= i <= N_GROUPS:
                 c_t = cpool.tile([P, GROUP * P], U32, name="c_t", align_bytes=64)
                 s_t = cpool.tile([P, GROUP * P], U8, name="s_t", align_bytes=64)
                 codes[i - 1] = c_t
                 scales[i - 1] = s_t
-                quantise(grouped[i - 1][:].rearrange("p a m u -> p (a m u)").bitcast(BF16), c_t, s_t)
+                quantise(flat_bf16(grouped[i - 1]), c_t, s_t)
                 if i == 1:
                     quantise(w_g[:].rearrange("p c t -> p (c t)"), w_codes, w_scl)
-                reciprocals(i - 1)
+            for b in PE_BATCHES:
+                if i - 1 in b:
+                    partial_degrees(i - 1, b)
+                    busy += 1
+                if i - 2 == b[-1]:
+                    fold_degrees(b)
+                if i - 3 == b[-1]:
+                    lo = GROUP * b[0]
+                    n = GROUP * len(b)
+                    nc.vector.tensor_scalar_add(
+                        out=degp1[:, lo : lo + n], in0=fixed[b[0]][:, 0, 0:n], scalar1=1.0
+                    )
+                    nc.vector.reciprocal(out=recip[:, lo : lo + n], in_=degp1[:, lo : lo + n])
+            for g in waiting:
+                lo = GROUP * g
+                nc.vector.reciprocal(out=recip[:, lo : lo + GROUP], in_=degp1[:, lo : lo + GROUP])
+            waiting = []
             if i == 2:
                 nc.vector.tensor_tensor(
                     out=h_g[:],
@@ -213,10 +298,13 @@ def tile_allgnn_pa_t_kernel(tc, x, adj, W_in, b_in, out):
                     in1=bias_sb[:].unsqueeze(2).to_broadcast([P, P, 4]),
                     op=ALU.add,
                 )
-            if i < n_groups:
-                degree(i, range(0, 2))
+            for g, a in plan[i]:
+                degree_on_vector(g, a)
+                summed[g] = summed.get(g, 0) + 1
+                if summed[g] == GROUP:
+                    waiting.append(g)
             if i == 1:
-                quantise(x_g[:].rearrange("p a m u -> p (a m u)").bitcast(BF16), x_codes, x_scl)
+                quantise(flat_bf16(x_g), x_codes, x_scl)
                 h_ps = ops.tile([P, GROUP, P], F32, name="o_t")
                 for t in range(4):
                     cols = slice(t * P, (t + 1) * P)
@@ -232,8 +320,10 @@ def tile_allgnn_pa_t_kernel(tc, x, adj, W_in, b_in, out):
                 acc["h"] = h_ps
             if i == 2:
                 quantise(h_g[:].rearrange("p c t -> p (c t)"), h_codes, h_scl)
-            if i < n_groups:
-                degree(i, range(2, GROUP))
-            if i >= LAG_MX:
-                multiply(i - LAG_MX)
-                finish(i - LAG_MX)
+            if i >= LAG:
+                multiply(i - LAG)
+                finish(i - LAG)
+                busy += 1
+            if i < N_GROUPS:
+                for w in range(2 - busy):
+                    idle_pass()

@@ -19,9 +19,8 @@ CHUNK_TILES = [4, 4] + [8] * 11
 GROUP = 4
 N_GROUPS = 24
 LAG = 6
-PE_BATCHES = ((0, 1, 2, 3), (12, 13, 14, 15))
+PE_BATCHES = ((4, 5, 6, 7), (14, 15, 16, 17))
 V_OUT = (5, 10, 15, 20, 22, 23)
-DEG_PER_ROUND = 3
 DEG_N = 32
 WARM = 3
 
@@ -33,7 +32,7 @@ def degree_plan():
     k = 0
     for i in range(N_GROUPS + LAG):
         now = []
-        while len(now) < DEG_PER_ROUND and k < len(todo) and todo[k][0] <= i + i // 3:
+        while len(now) < (2 if i < LAG else 3) and k < len(todo) and todo[k][0] <= i + i // 3:
             now.append(todo[k])
             k += 1
         plan.append(now)
@@ -265,7 +264,6 @@ def tile_allgnn_pa_t_kernel(tc, x, adj, W_in, b_in, out):
                 nc.scalar.copy(out=bias_sb[:], in_=b_ps[:, 0, :])
                 word_transposes("x", lambda j: x_sb[:, j, :])
                 evacuate("x", x_g)
-                nc.vector.tensor_copy(out=w_g[:], in_=w_sb[:].rearrange("p t c -> p c t"))
             if 1 <= i <= N_GROUPS:
                 c_t = cpool.tile([P, GROUP * P], U32, name="c_t", align_bytes=64)
                 s_t = cpool.tile([P, GROUP * P], U8, name="s_t", align_bytes=64)
@@ -303,6 +301,8 @@ def tile_allgnn_pa_t_kernel(tc, x, adj, W_in, b_in, out):
                 summed[g] = summed.get(g, 0) + 1
                 if summed[g] == GROUP:
                     waiting.append(g)
+            if i == 0:
+                nc.vector.tensor_copy(out=w_g[:], in_=w_sb[:].rearrange("p t c -> p c t"))
             if i == 1:
                 quantise(flat_bf16(x_g), x_codes, x_scl)
                 h_ps = ops.tile([P, GROUP, P], F32, name="o_t")
@@ -325,5 +325,5 @@ def tile_allgnn_pa_t_kernel(tc, x, adj, W_in, b_in, out):
                 finish(i - LAG)
                 busy += 1
             if i < N_GROUPS:
-                for w in range(2 - busy):
+                for w in range((1 if i < LAG else 2) - busy):
                     idle_pass()

@@ -5,6 +5,7 @@ from concourse.masks import make_identity
 
 F32 = mybir.dt.float32
 BF16 = mybir.dt.bfloat16
+I32 = mybir.dt.int32
 U32 = mybir.dt.uint32
 U8 = mybir.dt.uint8
 FP8X4 = mybir.dt.float8_e4m3fn_x4
@@ -22,7 +23,6 @@ LAG = 6
 PE_BATCHES = ((4, 5, 6, 7), (14, 15, 16, 17))
 V_OUT = (5, 10, 15, 20, 22, 23)
 DEG_N = 32
-WARM = 3
 
 
 def degree_plan():
@@ -61,7 +61,7 @@ def tile_allgnn_pa_t_kernel(tc, x, adj, W_in, b_in, out):
         nc.vector.memset(bz[:], 0.0)
         nc.scalar.dma_start(out=bz[0:1, :], in_=b_in.unsqueeze(0))
         zsrc = const.tile([P, 2048], BF16, align_bytes=64)
-        nc.vector.memset(zsrc[:], 0.0)
+        nc.vector.memset(zsrc[:].bitcast(I32), 0)
         nc.vector.quantize_mx(out=zc[:].bitcast(FP8X4), scales=zs[:], in_=zsrc[:])
         idle_ps = dps.tile([P, 512], F32, name="idle_ps")
 
@@ -75,9 +75,6 @@ def tile_allgnn_pa_t_kernel(tc, x, adj, W_in, b_in, out):
                 start=True,
                 stop=True,
             )
-
-        for w in range(WARM):
-            idle_pass()
 
         ident = const.tile([P, P], F32)
         make_identity(nc, ident[:])
@@ -100,9 +97,10 @@ def tile_allgnn_pa_t_kernel(tc, x, adj, W_in, b_in, out):
         row0 = 0
         for ci, nt in enumerate(CHUNK_TILES):
             a_t = const.tile([P, nt, 512], BF16, name="adj%d" % ci)
-            nc.sync.dma_start(
-                out=a_t[:], in_=adj[row0 : row0 + P * nt, :].rearrange("(p t) k -> p t k", t=nt)
-            )
+            a_src = adj[row0 : row0 + P * nt, :].rearrange("(p t) k -> p t k", t=nt)
+            cuts = (0, 2, 4) if ci == 0 else (0, nt)
+            for lo, hi in zip(cuts[:-1], cuts[1:]):
+                nc.sync.dma_start(out=a_t[:, lo:hi, :], in_=a_src[:, lo:hi, :])
             adj_sb.append(a_t)
             out_dst.append(out[row0 : row0 + P * nt, :].rearrange("(p t) c -> p t c", t=nt))
             for t0 in range(0, nt, GROUP):
@@ -285,10 +283,10 @@ def tile_allgnn_pa_t_kernel(tc, x, adj, W_in, b_in, out):
                         out=degp1[:, lo : lo + n], in0=fixed[b[0]][:, 0, 0:n], scalar1=1.0
                     )
                     nc.vector.reciprocal(out=recip[:, lo : lo + n], in_=degp1[:, lo : lo + n])
-            for g in waiting:
-                lo = GROUP * g
-                nc.vector.reciprocal(out=recip[:, lo : lo + GROUP], in_=degp1[:, lo : lo + GROUP])
-            waiting = []
+            if len(waiting) == 2:
+                lo = GROUP * waiting[0]
+                nc.vector.reciprocal(out=recip[:, lo : lo + 2 * GROUP], in_=degp1[:, lo : lo + 2 * GROUP])
+                waiting = []
             if i == 2:
                 nc.vector.tensor_tensor(
                     out=h_g[:],
@@ -325,5 +323,5 @@ def tile_allgnn_pa_t_kernel(tc, x, adj, W_in, b_in, out):
                 finish(i - LAG)
                 busy += 1
             if i < N_GROUPS:
-                for w in range((1 if i < LAG else 2) - busy):
+                for w in range((1 if 0 < i < LAG else 2) - busy):
                     idle_pass()

@@ -20,30 +20,16 @@ CHUNK_TILES = [4, 4] + [8] * 11
 GROUP = 4
 N_GROUPS = 24
 LAG = 6
-PE_BATCHES = ((4, 5, 6, 7), (14, 15, 16, 17))
-V_OUT = (5, 10, 15, 20, 22, 23)
-DEG_N = 32
-
-
-def degree_plan():
-    on_pe = [g for b in PE_BATCHES for g in b]
-    todo = [(g, a) for g in range(N_GROUPS) if g not in on_pe for a in range(GROUP)]
-    plan = []
-    k = 0
-    for i in range(N_GROUPS + LAG):
-        now = []
-        while len(now) < (2 if i < LAG else 3) and k < len(todo) and todo[k][0] <= i + i // 3:
-            now.append(todo[k])
-            k += 1
-        plan.append(now)
-    assert k == len(todo)
-    return plan
+BATCH = 4
+PE_TILES = 2
+V_TILES = GROUP - PE_TILES
+V_OUT = tuple(range(1, N_GROUPS, 2))
+DEG_N = 24
+IDLE_N = 256
 
 
 def tile_allgnn_pa_t_kernel(tc, x, adj, W_in, b_in, out):
     nc = tc.nc
-    on_pe = [g for b in PE_BATCHES for g in b]
-    plan = degree_plan()
     with ExitStack() as ctx:
         ctx.enter_context(tc.manual_schedule())
         const = ctx.enter_context(tc.tile_pool(name="const", bufs=1))
@@ -63,15 +49,15 @@ def tile_allgnn_pa_t_kernel(tc, x, adj, W_in, b_in, out):
         zsrc = const.tile([P, 2048], BF16, align_bytes=64)
         nc.vector.memset(zsrc[:].bitcast(I32), 0)
         nc.vector.quantize_mx(out=zc[:].bitcast(FP8X4), scales=zs[:], in_=zsrc[:])
-        idle_ps = dps.tile([P, 512], F32, name="idle_ps")
+        idle_ps = dps.tile([P, IDLE_N], F32, name="idle_ps")
 
         def idle_pass():
             nc.tensor.matmul_mx(
                 out=idle_ps[:],
                 lhsT=zc[:, 0:P].bitcast(FP8X4),
                 lhsT_scale=zs[:, 0:P],
-                rhs=zc[:].bitcast(FP8X4),
-                rhs_scale=zs[:],
+                rhs=zc[:, 0:IDLE_N].bitcast(FP8X4),
+                rhs_scale=zs[:, 0:IDLE_N],
                 start=True,
                 stop=True,
             )
@@ -80,15 +66,6 @@ def tile_allgnn_pa_t_kernel(tc, x, adj, W_in, b_in, out):
         make_identity(nc, ident[:])
         ones = const.tile([P, P], BF16)
         nc.vector.memset(ones[:], 1.0)
-        quad = const.tile([P, 32], F32)
-        nc.vector.tensor_reduce(
-            out=quad[:], in_=ident[:].rearrange("p (m t) -> p m t", t=4), axis=AX.X, op=ALU.add
-        )
-        sel = const.tile([P, 4, P], F32)
-        nc.vector.memset(sel[:], 0.0)
-        for j in range(4):
-            nc.vector.tensor_copy(out=sel[:, j, 32 * j : 32 * j + 32], in_=quad[:])
-
         adj_sb = []
         out_dst = []
         place = []
@@ -116,8 +93,8 @@ def tile_allgnn_pa_t_kernel(tc, x, adj, W_in, b_in, out):
                     in_=W_in.rearrange("(u p e) c -> p u e c", u=2, p=P, e=2),
                 )
 
-        degp1 = const.tile([P, 96], F32)
-        recip = const.tile([P, 96], F32)
+        degp1 = const.tile([P, N_GROUPS, GROUP], F32)
+        recip = const.tile([P, N_GROUPS, GROUP], F32)
         bias_sb = const.tile([P, P], F32)
         w_g = const.tile([P, P, 4], BF16, align_bytes=64)
         w_codes = const.tile([P, P], U32, align_bytes=64)
@@ -128,17 +105,13 @@ def tile_allgnn_pa_t_kernel(tc, x, adj, W_in, b_in, out):
         h_g = const.tile([P, P, 4], BF16, align_bytes=64)
         h_codes = const.tile([P, P], U32, align_bytes=64)
         h_scl = const.tile([P, P], U8, align_bytes=64)
-        part = {}
-        for b in PE_BATCHES:
-            p_t = const.tile([P, 4, GROUP * len(b)], F32, name="part%d" % b[0])
-            part[b[0]] = p_t
 
         banks = {}
         grouped = {}
         codes = {}
         scales = {}
         acc = {}
-        fixed = {}
+        sums = {}
 
         def word_transposes(key, rows_of):
             pair = []
@@ -169,7 +142,6 @@ def tile_allgnn_pa_t_kernel(tc, x, adj, W_in, b_in, out):
             return t4[:].rearrange("p a m u -> p (a m u)").bitcast(BF16)
 
         def degree_on_vector(g, a):
-            col = GROUP * g + a
             junk_v = jpool.tile([P, 512], BF16, name="junk_v")
             nc.vector.tensor_scalar(
                 out=junk_v[:],
@@ -178,38 +150,32 @@ def tile_allgnn_pa_t_kernel(tc, x, adj, W_in, b_in, out):
                 scalar2=1.0,
                 op0=ALU.mult,
                 op1=ALU.add,
-                accum_out=degp1[:, col : col + 1],
+                accum_out=degp1[:, g, a : a + 1],
             )
 
-        def partial_degrees(g, b):
-            d_t = dps.tile([P, 4 * GROUP, DEG_N], F32, name="d_t")
-            src = flat_bf16(grouped[g])
-            for s in range(4 * GROUP):
-                nc.tensor.matmul(
-                    out=d_t[:, s, :],
-                    lhsT=src[:, s * P : (s + 1) * P],
-                    rhs=ones[:, 0:DEG_N],
-                    start=True,
-                    stop=True,
-                )
-            lo = GROUP * (g - b[0])
-            nc.scalar.copy(
-                out=part[b[0]][:, :, lo : lo + GROUP],
-                in_=d_t[:, :, 0].rearrange("p (a j) -> p j a", j=4),
-            )
+        def degrees_on_tensor(g):
+            b, gb = divmod(g, BATCH)
+            if gb == 0:
+                d_t = dps.tile([P, BATCH, PE_TILES, DEG_N], F32, name="d_t")
+                sums[b] = d_t
+            cols = flat_bf16(grouped[g])
+            for e in range(PE_TILES):
+                lo = (V_TILES + e) * 4 * P
+                for t in range(4):
+                    nc.tensor.matmul(
+                        out=sums[b][:, gb, e, :],
+                        lhsT=cols[:, lo + t : lo + 4 * P : 4],
+                        rhs=ones[:, 0:DEG_N],
+                        start=(t == 0),
+                        stop=(t == 3),
+                    )
 
-        def fold_degrees(b):
-            n = GROUP * len(b)
-            d_t = dps.tile([P, 4 * GROUP, DEG_N], F32, name="d_t")
-            for j in range(4):
-                nc.tensor.matmul(
-                    out=d_t[:, 0, 0:n],
-                    lhsT=sel[:, j, :],
-                    rhs=part[b[0]][:, j, :],
-                    start=(j == 0),
-                    stop=(j == 3),
-                )
-            fixed[b[0]] = d_t
+        def reciprocals(b):
+            gs = slice(b * BATCH, (b + 1) * BATCH)
+            nc.vector.tensor_scalar_add(
+                out=degp1[:, gs, V_TILES:GROUP], in0=sums[b][:, :, :, 0], scalar1=1.0
+            )
+            nc.vector.reciprocal(out=recip[:, gs, :], in_=degp1[:, gs, :])
 
         def multiply(g):
             o_t = ops.tile([P, GROUP, P], F32, name="o_t")
@@ -228,13 +194,12 @@ def tile_allgnn_pa_t_kernel(tc, x, adj, W_in, b_in, out):
 
         def finish(g):
             ci, t0 = place[g]
-            lo = GROUP * g
             res = rpool.tile([P, GROUP, P], F32, name="res")
             if g in V_OUT:
                 nc.vector.tensor_tensor(
                     out=res[:],
                     in0=acc[g][:],
-                    in1=recip[:, lo : lo + GROUP].unsqueeze(2).to_broadcast([P, GROUP, P]),
+                    in1=recip[:, g, :].unsqueeze(2).to_broadcast([P, GROUP, P]),
                     op=ALU.mult,
                 )
             else:
@@ -243,14 +208,11 @@ def tile_allgnn_pa_t_kernel(tc, x, adj, W_in, b_in, out):
                         out=res[:, a, :],
                         in_=acc[g][:, a, :],
                         func=ACT.Copy,
-                        scale=recip[:, lo + a : lo + a + 1],
+                        scale=recip[:, g, a : a + 1],
                     )
             nc.sync.dma_start(out=out_dst[ci][:, t0 : t0 + GROUP, :], in_=res[:])
 
-        summed = {}
-        waiting = []
         for i in range(N_GROUPS + LAG):
-            busy = 0
             if i < N_GROUPS:
                 word_transposes(i, adj_rows(i))
                 g_t = gpool.tile([P, GROUP, P, 2], F32, name="g_t", align_bytes=64)
@@ -262,6 +224,8 @@ def tile_allgnn_pa_t_kernel(tc, x, adj, W_in, b_in, out):
                 nc.scalar.copy(out=bias_sb[:], in_=b_ps[:, 0, :])
                 word_transposes("x", lambda j: x_sb[:, j, :])
                 evacuate("x", x_g)
+            if i >= BATCH + 1 and (i - 1) % BATCH == 0 and i - 1 <= N_GROUPS:
+                reciprocals((i - 1) // BATCH - 1)
             if 1 <= i <= N_GROUPS:
                 c_t = cpool.tile([P, GROUP * P], U32, name="c_t", align_bytes=64)
                 s_t = cpool.tile([P, GROUP * P], U8, name="s_t", align_bytes=64)
@@ -270,23 +234,8 @@ def tile_allgnn_pa_t_kernel(tc, x, adj, W_in, b_in, out):
                 quantise(flat_bf16(grouped[i - 1]), c_t, s_t)
                 if i == 1:
                     quantise(w_g[:].rearrange("p c t -> p (c t)"), w_codes, w_scl)
-            for b in PE_BATCHES:
-                if i - 1 in b:
-                    partial_degrees(i - 1, b)
-                    busy += 1
-                if i - 2 == b[-1]:
-                    fold_degrees(b)
-                if i - 3 == b[-1]:
-                    lo = GROUP * b[0]
-                    n = GROUP * len(b)
-                    nc.vector.tensor_scalar_add(
-                        out=degp1[:, lo : lo + n], in0=fixed[b[0]][:, 0, 0:n], scalar1=1.0
-                    )
-                    nc.vector.reciprocal(out=recip[:, lo : lo + n], in_=degp1[:, lo : lo + n])
-            if len(waiting) == 2:
-                lo = GROUP * waiting[0]
-                nc.vector.reciprocal(out=recip[:, lo : lo + 2 * GROUP], in_=degp1[:, lo : lo + 2 * GROUP])
-                waiting = []
+            if 1 <= i <= N_GROUPS:
+                degrees_on_tensor(i - 1)
             if i == 2:
                 nc.vector.tensor_tensor(
                     out=h_g[:],
@@ -294,11 +243,9 @@ def tile_allgnn_pa_t_kernel(tc, x, adj, W_in, b_in, out):
                     in1=bias_sb[:].unsqueeze(2).to_broadcast([P, P, 4]),
                     op=ALU.add,
                 )
-            for g, a in plan[i]:
-                degree_on_vector(g, a)
-                summed[g] = summed.get(g, 0) + 1
-                if summed[g] == GROUP:
-                    waiting.append(g)
+            if i < N_GROUPS:
+                for a in range(V_TILES):
+                    degree_on_vector(i, a)
             if i == 0:
                 nc.vector.tensor_copy(out=w_g[:], in_=w_sb[:].rearrange("p t c -> p c t"))
             if i == 1:
@@ -321,7 +268,6 @@ def tile_allgnn_pa_t_kernel(tc, x, adj, W_in, b_in, out):
             if i >= LAG:
                 multiply(i - LAG)
                 finish(i - LAG)
-                busy += 1
             if i < N_GROUPS:
-                for w in range((1 if 0 < i < LAG else 2) - busy):
+                for w in range(3 if i < LAG else 1):
                     idle_pass()

@@ -19,13 +19,14 @@ FLOPS = 2 * 12288 * 512 * 128 + 2 * 512 * 512 * 128
 CHUNK_TILES = [4, 4] + [8] * 11
 GROUP = 4
 N_GROUPS = 24
-LAG = 6
-BATCH = 4
+LAG = 3
+FIRST_PRODUCT = 5
+LAST_ROUND = N_GROUPS + 1
+BATCH = 2
 PE_TILES = 2
 V_TILES = GROUP - PE_TILES
 V_OUT = tuple(range(1, N_GROUPS, 2))
 DEG_N = 24
-IDLE_N = 256
 
 
 def tile_allgnn_pa_t_kernel(tc, x, adj, W_in, b_in, out):
@@ -34,34 +35,16 @@ def tile_allgnn_pa_t_kernel(tc, x, adj, W_in, b_in, out):
         ctx.enter_context(tc.manual_schedule())
         const = ctx.enter_context(tc.tile_pool(name="const", bufs=1))
         gpool = ctx.enter_context(tc.tile_pool(name="grouped", bufs=4))
-        cpool = ctx.enter_context(tc.tile_pool(name="codes", bufs=LAG + 3))
+        cpool = ctx.enter_context(tc.tile_pool(name="codes", bufs=9))
         rpool = ctx.enter_context(tc.tile_pool(name="res", bufs=N_GROUPS))
         jpool = ctx.enter_context(tc.tile_pool(name="junk", bufs=4))
         tps = ctx.enter_context(tc.psum_pool(name="tps", bufs=4))
         ops = ctx.enter_context(tc.psum_pool(name="ops", bufs=2))
-        dps = ctx.enter_context(tc.psum_pool(name="dps", bufs=1))
+        dps = ctx.enter_context(tc.psum_pool(name="dps", bufs=2))
 
-        zc = const.tile([P, 512], U32, align_bytes=64)
-        zs = const.tile([P, 512], U8, align_bytes=64)
         bz = const.tile([P, P], BF16)
         nc.vector.memset(bz[:], 0.0)
         nc.scalar.dma_start(out=bz[0:1, :], in_=b_in.unsqueeze(0))
-        zsrc = const.tile([P, 2048], BF16, align_bytes=64)
-        nc.vector.memset(zsrc[:].bitcast(I32), 0)
-        nc.vector.quantize_mx(out=zc[:].bitcast(FP8X4), scales=zs[:], in_=zsrc[:])
-        idle_ps = dps.tile([P, IDLE_N], F32, name="idle_ps")
-
-        def idle_pass():
-            nc.tensor.matmul_mx(
-                out=idle_ps[:],
-                lhsT=zc[:, 0:P].bitcast(FP8X4),
-                lhsT_scale=zs[:, 0:P],
-                rhs=zc[:, 0:IDLE_N].bitcast(FP8X4),
-                rhs_scale=zs[:, 0:IDLE_N],
-                start=True,
-                stop=True,
-            )
-
         ident = const.tile([P, P], F32)
         make_identity(nc, ident[:])
         ones = const.tile([P, P], BF16)
@@ -212,7 +195,8 @@ def tile_allgnn_pa_t_kernel(tc, x, adj, W_in, b_in, out):
                     )
             nc.sync.dma_start(out=out_dst[ci][:, t0 : t0 + GROUP, :], in_=res[:])
 
-        for i in range(N_GROUPS + LAG):
+        done = 0
+        for i in range(LAST_ROUND + 1):
             if i < N_GROUPS:
                 word_transposes(i, adj_rows(i))
                 g_t = gpool.tile([P, GROUP, P, 2], F32, name="g_t", align_bytes=64)
@@ -224,7 +208,7 @@ def tile_allgnn_pa_t_kernel(tc, x, adj, W_in, b_in, out):
                 nc.scalar.copy(out=bias_sb[:], in_=b_ps[:, 0, :])
                 word_transposes("x", lambda j: x_sb[:, j, :])
                 evacuate("x", x_g)
-            if i >= BATCH + 1 and (i - 1) % BATCH == 0 and i - 1 <= N_GROUPS:
+            if i >= BATCH + 1 and (i - 1) % BATCH == 0:
                 reciprocals((i - 1) // BATCH - 1)
             if 1 <= i <= N_GROUPS:
                 c_t = cpool.tile([P, GROUP * P], U32, name="c_t", align_bytes=64)
@@ -265,9 +249,12 @@ def tile_allgnn_pa_t_kernel(tc, x, adj, W_in, b_in, out):
                 acc["h"] = h_ps
             if i == 2:
                 quantise(h_g[:].rearrange("p c t -> p (c t)"), h_codes, h_scl)
-            if i >= LAG:
-                multiply(i - LAG)
-                finish(i - LAG)
-            if i < N_GROUPS:
-                for w in range(3 if i < LAG else 1):
-                    idle_pass()
+            now = []
+            if i >= FIRST_PRODUCT:
+                ready = N_GROUPS if i == LAST_ROUND else i - LAG + 1
+                now = list(range(done, min(ready, done + 2)))
+                done += len(now)
+            for g in now:
+                multiply(g)
+            for g in now:
+                finish(g)

@@ -23,10 +23,10 @@ LAG = 3
 FIRST_PRODUCT = 5
 LAST_ROUND = N_GROUPS + 1
 BATCH = 2
-PE_TILES = 2
+PE_TILES = 3
 V_TILES = GROUP - PE_TILES
 V_OUT = tuple(range(1, N_GROUPS, 2))
-DEG_N = 24
+DEG_N = 16
 
 
 def tile_allgnn_pa_t_kernel(tc, x, adj, W_in, b_in, out):

@@ -16,17 +16,18 @@ AX = mybir.AxisListType
 P = 128
 FLOPS = 2 * 12288 * 512 * 128 + 2 * 512 * 512 * 128
 
-CHUNK_TILES = [4, 4] + [8] * 11
+CHUNK_TILES = [4] * 4 + [8] * 10
 GROUP = 4
 N_GROUPS = 24
 LAG = 3
-FIRST_PRODUCT = 5
-LAST_ROUND = N_GROUPS + 1
-BATCH = 2
+FIRST_PRODUCT = 4
 PE_TILES = 3
 V_TILES = GROUP - PE_TILES
 V_OUT = tuple(range(1, N_GROUPS, 2))
 DEG_N = 16
+IDLE_N = 256
+IDLE_BEFORE = 6
+IDLE_HEAD = 3
 
 
 def tile_allgnn_pa_t_kernel(tc, x, adj, W_in, b_in, out):
@@ -45,6 +46,25 @@ def tile_allgnn_pa_t_kernel(tc, x, adj, W_in, b_in, out):
         bz = const.tile([P, P], BF16)
         nc.vector.memset(bz[:], 0.0)
         nc.scalar.dma_start(out=bz[0:1, :], in_=b_in.unsqueeze(0))
+        zc = const.tile([P, IDLE_N], U32, align_bytes=64)
+        zs = const.tile([P, IDLE_N], U8, align_bytes=64)
+        zsrc = const.tile([P, 4 * IDLE_N], BF16, align_bytes=64)
+        nc.vector.memset(zsrc[:].bitcast(I32), 0)
+        nc.vector.quantize_mx(out=zc[:].bitcast(FP8X4), scales=zs[:], in_=zsrc[:])
+
+        def idle_passes(n):
+            idle_t = dps.tile([P, IDLE_N], F32, name="d_t")
+            for w in range(n):
+                nc.tensor.matmul_mx(
+                    out=idle_t[:],
+                    lhsT=zc[:, 0:P].bitcast(FP8X4),
+                    lhsT_scale=zs[:, 0:P],
+                    rhs=zc[:].bitcast(FP8X4),
+                    rhs_scale=zs[:],
+                    start=True,
+                    stop=True,
+                )
+
         ident = const.tile([P, P], F32)
         make_identity(nc, ident[:])
         ones = const.tile([P, P], BF16)
@@ -137,27 +157,26 @@ def tile_allgnn_pa_t_kernel(tc, x, adj, W_in, b_in, out):
             )
 
         def degrees_on_tensor(g):
-            b, gb = divmod(g, BATCH)
-            if gb == 0:
-                d_t = dps.tile([P, BATCH, PE_TILES, DEG_N], F32, name="d_t")
-                sums[b] = d_t
+            d_t = dps.tile([P, PE_TILES, DEG_N], F32, name="d_t")
+            sums[g] = d_t
             cols = flat_bf16(grouped[g])
             for e in range(PE_TILES):
                 lo = (V_TILES + e) * 4 * P
                 for t in range(4):
                     nc.tensor.matmul(
-                        out=sums[b][:, gb, e, :],
+                        out=d_t[:, e, :],
                         lhsT=cols[:, lo + t : lo + 4 * P : 4],
                         rhs=ones[:, 0:DEG_N],
                         start=(t == 0),
                         stop=(t == 3),
                     )
 
-        def reciprocals(b):
-            gs = slice(b * BATCH, (b + 1) * BATCH)
+        def add_one(g):
             nc.vector.tensor_scalar_add(
-                out=degp1[:, gs, V_TILES:GROUP], in0=sums[b][:, :, :, 0], scalar1=1.0
+                out=degp1[:, g, V_TILES:GROUP], in0=sums[g][:, :, 0], scalar1=1.0
             )
+
+        def invert(gs):
             nc.vector.reciprocal(out=recip[:, gs, :], in_=degp1[:, gs, :])
 
         def multiply(g):
@@ -195,45 +214,25 @@ def tile_allgnn_pa_t_kernel(tc, x, adj, W_in, b_in, out):
                     )
             nc.sync.dma_start(out=out_dst[ci][:, t0 : t0 + GROUP, :], in_=res[:])
 
+        idle_passes(IDLE_BEFORE)
         done = 0
-        for i in range(LAST_ROUND + 1):
+        for i in range(N_GROUPS + 1):
             if i < N_GROUPS:
                 word_transposes(i, adj_rows(i))
                 g_t = gpool.tile([P, GROUP, P, 2], F32, name="g_t", align_bytes=64)
                 grouped[i] = g_t
                 evacuate(i, g_t)
             if i == 0:
+                word_transposes("x", lambda j: x_sb[:, j, :])
+                evacuate("x", x_g)
+                degree_on_vector(0, 0)
+                nc.vector.tensor_copy(out=w_g[:], in_=w_sb[:].rearrange("p t c -> p c t"))
+                quantise(w_g[:].rearrange("p c t -> p (c t)"), w_codes, w_scl)
+                quantise(flat_bf16(x_g), x_codes, x_scl)
+            if i == 1:
                 b_ps = ops.tile([P, GROUP, P], F32, name="o_t")
                 nc.tensor.matmul(out=b_ps[:, 0, :], lhsT=ones[:], rhs=bz[:], start=True, stop=True)
                 nc.scalar.copy(out=bias_sb[:], in_=b_ps[:, 0, :])
-                word_transposes("x", lambda j: x_sb[:, j, :])
-                evacuate("x", x_g)
-            if i >= BATCH + 1 and (i - 1) % BATCH == 0:
-                reciprocals((i - 1) // BATCH - 1)
-            if 1 <= i <= N_GROUPS:
-                c_t = cpool.tile([P, GROUP * P], U32, name="c_t", align_bytes=64)
-                s_t = cpool.tile([P, GROUP * P], U8, name="s_t", align_bytes=64)
-                codes[i - 1] = c_t
-                scales[i - 1] = s_t
-                quantise(flat_bf16(grouped[i - 1]), c_t, s_t)
-                if i == 1:
-                    quantise(w_g[:].rearrange("p c t -> p (c t)"), w_codes, w_scl)
-            if 1 <= i <= N_GROUPS:
-                degrees_on_tensor(i - 1)
-            if i == 2:
-                nc.vector.tensor_tensor(
-                    out=h_g[:],
-                    in0=acc["h"][:].rearrange("p t c -> p c t"),
-                    in1=bias_sb[:].unsqueeze(2).to_broadcast([P, P, 4]),
-                    op=ALU.add,
-                )
-            if i < N_GROUPS:
-                for a in range(V_TILES):
-                    degree_on_vector(i, a)
-            if i == 0:
-                nc.vector.tensor_copy(out=w_g[:], in_=w_sb[:].rearrange("p t c -> p c t"))
-            if i == 1:
-                quantise(flat_bf16(x_g), x_codes, x_scl)
                 h_ps = ops.tile([P, GROUP, P], F32, name="o_t")
                 for t in range(4):
                     cols = slice(t * P, (t + 1) * P)
@@ -247,14 +246,39 @@ def tile_allgnn_pa_t_kernel(tc, x, adj, W_in, b_in, out):
                         stop=True,
                     )
                 acc["h"] = h_ps
+            if i >= 1:
+                degrees_on_tensor(i - 1)
+                c_t = cpool.tile([P, GROUP * P], U32, name="c_t", align_bytes=64)
+                s_t = cpool.tile([P, GROUP * P], U8, name="s_t", align_bytes=64)
+                codes[i - 1] = c_t
+                scales[i - 1] = s_t
+                quantise(flat_bf16(grouped[i - 1]), c_t, s_t)
+            if i == 1:
+                nc.vector.tensor_tensor(
+                    out=h_g[:],
+                    in0=acc["h"][:].rearrange("p t c -> p c t"),
+                    in1=bias_sb[:].unsqueeze(2).to_broadcast([P, P, 4]),
+                    op=ALU.add,
+                )
             if i == 2:
                 quantise(h_g[:].rearrange("p c t -> p (c t)"), h_codes, h_scl)
+            if i >= 2:
+                add_one(i - 2)
+            if 1 <= i < N_GROUPS:
+                degree_on_vector(i, 0)
+            if i == N_GROUPS:
+                add_one(i - 1)
+                invert(slice(i - 2, i))
+            elif i >= 2:
+                invert(slice(i - 2, i - 1))
             now = []
             if i >= FIRST_PRODUCT:
-                ready = N_GROUPS if i == LAST_ROUND else i - LAG + 1
-                now = list(range(done, min(ready, done + 2)))
+                ready = N_GROUPS if i == N_GROUPS else i - LAG + 1
+                now = list(range(done, ready if i == N_GROUPS else min(ready, done + 2)))
                 done += len(now)
             for g in now:
                 multiply(g)
-            for g in now:
                 finish(g)
+            if i < FIRST_PRODUCT:
+                idle_passes(IDLE_HEAD)
+        assert done == N_GROUPS

@@ -19,11 +19,10 @@ FLOPS = 2 * 12288 * 512 * 128 + 2 * 512 * 512 * 128
 CHUNK_TILES = [4] * 4 + [8] * 10
 GROUP = 4
 N_GROUPS = 24
+LAST = N_GROUPS - 1
 LAG = 3
-FIRST_PRODUCT = 4
 PE_TILES = 3
-V_TILES = GROUP - PE_TILES
-V_OUT = tuple(range(1, N_GROUPS, 2))
+S_OUT = tuple(range(1, LAST, 3))
 DEG_N = 16
 IDLE_N = 256
 IDLE_BEFORE = 6
@@ -37,7 +36,7 @@ def tile_allgnn_pa_t_kernel(tc, x, adj, W_in, b_in, out):
         const = ctx.enter_context(tc.tile_pool(name="const", bufs=1))
         gpool = ctx.enter_context(tc.tile_pool(name="grouped", bufs=4))
         cpool = ctx.enter_context(tc.tile_pool(name="codes", bufs=9))
-        rpool = ctx.enter_context(tc.tile_pool(name="res", bufs=N_GROUPS))
+        rpool = ctx.enter_context(tc.tile_pool(name="res", bufs=N_GROUPS + 1))
         jpool = ctx.enter_context(tc.tile_pool(name="junk", bufs=4))
         tps = ctx.enter_context(tc.psum_pool(name="tps", bufs=4))
         ops = ctx.enter_context(tc.psum_pool(name="ops", bufs=2))
@@ -134,8 +133,8 @@ def tile_allgnn_pa_t_kernel(tc, x, adj, W_in, b_in, out):
                     in_=banks[key][half][:].rearrange("p a u m -> p a m u"),
                 )
 
-        def quantise(src_bf16, c_t, s_t):
-            nc.vector.quantize_mx(out=c_t[:].bitcast(FP8X4), scales=s_t[:], in_=src_bf16)
+        def quantise(src_bf16, c_ap, s_ap):
+            nc.vector.quantize_mx(out=c_ap.bitcast(FP8X4), scales=s_ap, in_=src_bf16)
 
         def adj_rows(g):
             ci, t0 = place[g]
@@ -143,6 +142,9 @@ def tile_allgnn_pa_t_kernel(tc, x, adj, W_in, b_in, out):
 
         def flat_bf16(t4):
             return t4[:].rearrange("p a m u -> p (a m u)").bitcast(BF16)
+
+        def v_tiles(g):
+            return 0 if g == LAST else GROUP - PE_TILES
 
         def degree_on_vector(g, a):
             junk_v = jpool.tile([P, 512], BF16, name="junk_v")
@@ -157,11 +159,12 @@ def tile_allgnn_pa_t_kernel(tc, x, adj, W_in, b_in, out):
             )
 
         def degrees_on_tensor(g):
-            d_t = dps.tile([P, PE_TILES, DEG_N], F32, name="d_t")
+            first = v_tiles(g)
+            d_t = dps.tile([P, GROUP - first, DEG_N], F32, name="d_t")
             sums[g] = d_t
             cols = flat_bf16(grouped[g])
-            for e in range(PE_TILES):
-                lo = (V_TILES + e) * 4 * P
+            for e in range(GROUP - first):
+                lo = (first + e) * 4 * P
                 for t in range(4):
                     nc.tensor.matmul(
                         out=d_t[:, e, :],
@@ -173,18 +176,17 @@ def tile_allgnn_pa_t_kernel(tc, x, adj, W_in, b_in, out):
 
         def add_one(g):
             nc.vector.tensor_scalar_add(
-                out=degp1[:, g, V_TILES:GROUP], in0=sums[g][:, :, 0], scalar1=1.0
+                out=degp1[:, g, v_tiles(g) : GROUP], in0=sums[g][:, :, 0], scalar1=1.0
             )
 
-        def invert(gs):
-            nc.vector.reciprocal(out=recip[:, gs, :], in_=degp1[:, gs, :])
+        def invert(g):
+            nc.vector.reciprocal(out=recip[:, g, :], in_=degp1[:, g, :])
 
-        def multiply(g):
-            o_t = ops.tile([P, GROUP, P], F32, name="o_t")
-            for a in range(GROUP):
+        def multiply(g, o_t, tiles):
+            for slot, a in enumerate(tiles):
                 cols = slice(a * P, (a + 1) * P)
                 nc.tensor.matmul_mx(
-                    out=o_t[:, a, :],
+                    out=o_t[:, slot, :],
                     lhsT=codes[g][:, cols].bitcast(FP8X4),
                     lhsT_scale=scales[g][:, cols],
                     rhs=h_codes[:].bitcast(FP8X4),
@@ -192,43 +194,42 @@ def tile_allgnn_pa_t_kernel(tc, x, adj, W_in, b_in, out):
                     start=True,
                     stop=True,
                 )
-            acc[g] = o_t
 
-        def finish(g):
+        def finish(g, o_t, tiles, on_scalar):
             ci, t0 = place[g]
+            n = len(tiles)
             res = rpool.tile([P, GROUP, P], F32, name="res")
-            if g in V_OUT:
-                nc.vector.tensor_tensor(
-                    out=res[:],
-                    in0=acc[g][:],
-                    in1=recip[:, g, :].unsqueeze(2).to_broadcast([P, GROUP, P]),
-                    op=ALU.mult,
-                )
-            else:
-                for a in range(GROUP):
+            if on_scalar:
+                for slot, a in enumerate(tiles):
                     nc.scalar.activation(
-                        out=res[:, a, :],
-                        in_=acc[g][:, a, :],
+                        out=res[:, slot, :],
+                        in_=o_t[:, slot, :],
                         func=ACT.Copy,
                         scale=recip[:, g, a : a + 1],
                     )
-            nc.sync.dma_start(out=out_dst[ci][:, t0 : t0 + GROUP, :], in_=res[:])
+            else:
+                nc.vector.tensor_tensor(
+                    out=res[:, 0:n, :],
+                    in0=o_t[:, 0:n, :],
+                    in1=recip[:, g, tiles[0] : tiles[0] + n].unsqueeze(2).to_broadcast([P, n, P]),
+                    op=ALU.mult,
+                )
+            row = t0 + tiles[0]
+            nc.sync.dma_start(out=out_dst[ci][:, row : row + n, :], in_=res[:, 0:n, :])
 
         idle_passes(IDLE_BEFORE)
-        done = 0
-        for i in range(N_GROUPS + 1):
-            if i < N_GROUPS:
-                word_transposes(i, adj_rows(i))
-                g_t = gpool.tile([P, GROUP, P, 2], F32, name="g_t", align_bytes=64)
-                grouped[i] = g_t
-                evacuate(i, g_t)
+        for i in range(N_GROUPS):
+            word_transposes(i, adj_rows(i))
+            g_t = gpool.tile([P, GROUP, P, 2], F32, name="g_t", align_bytes=64)
+            grouped[i] = g_t
+            evacuate(i, g_t)
             if i == 0:
                 word_transposes("x", lambda j: x_sb[:, j, :])
                 evacuate("x", x_g)
                 degree_on_vector(0, 0)
                 nc.vector.tensor_copy(out=w_g[:], in_=w_sb[:].rearrange("p t c -> p c t"))
-                quantise(w_g[:].rearrange("p c t -> p (c t)"), w_codes, w_scl)
-                quantise(flat_bf16(x_g), x_codes, x_scl)
+                quantise(w_g[:].rearrange("p c t -> p (c t)"), w_codes[:], w_scl[:])
+                quantise(flat_bf16(x_g), x_codes[:], x_scl[:])
             if i == 1:
                 b_ps = ops.tile([P, GROUP, P], F32, name="o_t")
                 nc.tensor.matmul(out=b_ps[:, 0, :], lhsT=ones[:], rhs=bz[:], start=True, stop=True)
@@ -252,7 +253,7 @@ def tile_allgnn_pa_t_kernel(tc, x, adj, W_in, b_in, out):
                 s_t = cpool.tile([P, GROUP * P], U8, name="s_t", align_bytes=64)
                 codes[i - 1] = c_t
                 scales[i - 1] = s_t
-                quantise(flat_bf16(grouped[i - 1]), c_t, s_t)
+                quantise(flat_bf16(grouped[i - 1]), c_t[:], s_t[:])
             if i == 1:
                 nc.vector.tensor_tensor(
                     out=h_g[:],
@@ -261,24 +262,45 @@ def tile_allgnn_pa_t_kernel(tc, x, adj, W_in, b_in, out):
                     op=ALU.add,
                 )
             if i == 2:
-                quantise(h_g[:].rearrange("p c t -> p (c t)"), h_codes, h_scl)
+                quantise(h_g[:].rearrange("p c t -> p (c t)"), h_codes[:], h_scl[:])
             if i >= 2:
                 add_one(i - 2)
-            if 1 <= i < N_GROUPS:
+            if 1 <= i < LAST:
                 degree_on_vector(i, 0)
-            if i == N_GROUPS:
-                add_one(i - 1)
-                invert(slice(i - 2, i))
-            elif i >= 2:
-                invert(slice(i - 2, i - 1))
-            now = []
-            if i >= FIRST_PRODUCT:
-                ready = N_GROUPS if i == N_GROUPS else i - LAG + 1
-                now = list(range(done, ready if i == N_GROUPS else min(ready, done + 2)))
-                done += len(now)
-            for g in now:
-                multiply(g)
-                finish(g)
-            if i < FIRST_PRODUCT:
+            if i >= 2:
+                invert(i - 2)
+            if i >= LAG:
+                o_t = ops.tile([P, GROUP, P], F32, name="o_t")
+                multiply(i - LAG, o_t, range(GROUP))
+                finish(i - LAG, o_t, range(GROUP), i - LAG in S_OUT)
+            else:
                 idle_passes(IDLE_HEAD)
-        assert done == N_GROUPS
+
+        halves = (range(0, 2), range(2, GROUP))
+        c_t = cpool.tile([P, GROUP * P], U32, name="c_t", align_bytes=64)
+        s_t = cpool.tile([P, GROUP * P], U8, name="s_t", align_bytes=64)
+        codes[LAST] = c_t
+        scales[LAST] = s_t
+
+        def quantise_half(half):
+            cols = slice(2 * P * half, 2 * P * (half + 1))
+            words = slice(8 * P * half, 8 * P * (half + 1))
+            quantise(flat_bf16(grouped[LAST])[:, words], c_t[:, cols], s_t[:, cols])
+
+        o_21 = ops.tile([P, GROUP, P], F32, name="o_t")
+        multiply(LAST - 2, o_21, range(GROUP))
+        add_one(LAST - 1)
+        quantise_half(0)
+        invert(LAST - 1)
+        finish(LAST - 2, o_21, range(GROUP), False)
+        o_22 = tps.tile([P, GROUP, P], F32, name="tp")
+        multiply(LAST - 1, o_22, range(GROUP))
+        finish(LAST - 1, o_22, range(GROUP), True)
+        degrees_on_tensor(LAST)
+        quantise_half(1)
+        add_one(LAST)
+        invert(LAST)
+        for half in range(2):
+            o_h = tps.tile([P, GROUP, P], F32, name="tp")
+            multiply(LAST, o_h, halves[half])
+            finish(LAST, o_h, halves[half], half == 1)

from contextlib import ExitStack

import concourse.mybir as mybir
from concourse.masks import make_identity

F32 = mybir.dt.float32
BF16 = mybir.dt.bfloat16
I32 = mybir.dt.int32
U32 = mybir.dt.uint32
U8 = mybir.dt.uint8
FP8X4 = mybir.dt.float8_e4m3fn_x4
ALU = mybir.AluOpType
ACT = mybir.ActivationFunctionType
AX = mybir.AxisListType

P = 128
FLOPS = 2 * 12288 * 512 * 128 + 2 * 512 * 512 * 128

CHUNK_TILES = [4] * 4 + [8] * 10
GROUP = 4
N_GROUPS = 24
LAST = N_GROUPS - 1
LAG = 3
PE_TILES = 3
S_OUT = tuple(range(1, LAST, 3))
DEG_N = 16
IDLE_N = 256
IDLE_BEFORE = 6
IDLE_HEAD = 3


def tile_allgnn_pa_t_kernel(tc, x, adj, W_in, b_in, out):
    nc = tc.nc
    with ExitStack() as ctx:
        ctx.enter_context(tc.manual_schedule())
        const = ctx.enter_context(tc.tile_pool(name="const", bufs=1))
        gpool = ctx.enter_context(tc.tile_pool(name="grouped", bufs=4))
        cpool = ctx.enter_context(tc.tile_pool(name="codes", bufs=9))
        rpool = ctx.enter_context(tc.tile_pool(name="res", bufs=N_GROUPS + 1))
        jpool = ctx.enter_context(tc.tile_pool(name="junk", bufs=4))
        tps = ctx.enter_context(tc.psum_pool(name="tps", bufs=4))
        ops = ctx.enter_context(tc.psum_pool(name="ops", bufs=2))
        dps = ctx.enter_context(tc.psum_pool(name="dps", bufs=2))

        bz = const.tile([P, P], BF16)
        nc.vector.memset(bz[:], 0.0)
        nc.scalar.dma_start(out=bz[0:1, :], in_=b_in.unsqueeze(0))
        zc = const.tile([P, IDLE_N], U32, align_bytes=64)
        zs = const.tile([P, IDLE_N], U8, align_bytes=64)
        zsrc = const.tile([P, 4 * IDLE_N], BF16, align_bytes=64)
        nc.vector.memset(zsrc[:].bitcast(I32), 0)
        nc.vector.quantize_mx(out=zc[:].bitcast(FP8X4), scales=zs[:], in_=zsrc[:])

        def idle_passes(n):
            idle_t = dps.tile([P, IDLE_N], F32, name="d_t")
            for w in range(n):
                nc.tensor.matmul_mx(
                    out=idle_t[:],
                    lhsT=zc[:, 0:P].bitcast(FP8X4),
                    lhsT_scale=zs[:, 0:P],
                    rhs=zc[:].bitcast(FP8X4),
                    rhs_scale=zs[:],
                    start=True,
                    stop=True,
                )

        ident = const.tile([P, P], F32)
        make_identity(nc, ident[:])
        ones = const.tile([P, P], BF16)
        nc.vector.memset(ones[:], 1.0)
        adj_sb = []
        out_dst = []
        place = []
        x_sb = const.tile([P, 4, 512], BF16)
        w_sb = const.tile([P, 4, P], BF16)
        row0 = 0
        for ci, nt in enumerate(CHUNK_TILES):
            a_t = const.tile([P, nt, 512], BF16, name="adj%d" % ci)
            a_src = adj[row0 : row0 + P * nt, :].rearrange("(p t) k -> p t k", t=nt)
            cuts = (0, 2, 4) if ci == 0 else (0, nt)
            for lo, hi in zip(cuts[:-1], cuts[1:]):
                nc.sync.dma_start(out=a_t[:, lo:hi, :], in_=a_src[:, lo:hi, :])
            adj_sb.append(a_t)
            out_dst.append(out[row0 : row0 + P * nt, :].rearrange("(p t) c -> p t c", t=nt))
            for t0 in range(0, nt, GROUP):
                place.append((ci, t0))
            row0 += P * nt
            if ci == 0:
                nc.sync.dma_start(
                    out=x_sb[:].rearrange("p (u e) f -> p u e f", u=2),
                    in_=x.rearrange("(u p e) f -> p u e f", u=2, p=P, e=2),
                )
                nc.sync.dma_start(
                    out=w_sb[:].rearrange("p (u e) c -> p u e c", u=2),
                    in_=W_in.rearrange("(u p e) c -> p u e c", u=2, p=P, e=2),
                )

        degp1 = const.tile([P, N_GROUPS, GROUP], F32)
        recip = const.tile([P, N_GROUPS, GROUP], F32)
        bias_sb = const.tile([P, P], F32)
        w_g = const.tile([P, P, 4], BF16, align_bytes=64)
        w_codes = const.tile([P, P], U32, align_bytes=64)
        w_scl = const.tile([P, P], U8, align_bytes=64)
        x_g = const.tile([P, 4, P, 2], F32, align_bytes=64)
        x_codes = const.tile([P, 4 * P], U32, align_bytes=64)
        x_scl = const.tile([P, 4 * P], U8, align_bytes=64)
        h_g = const.tile([P, P, 4], BF16, align_bytes=64)
        h_codes = const.tile([P, P], U32, align_bytes=64)
        h_scl = const.tile([P, P], U8, align_bytes=64)

        banks = {}
        grouped = {}
        codes = {}
        scales = {}
        acc = {}
        sums = {}

        def word_transposes(key, rows_of):
            pair = []
            for half in range(2):
                tp = tps.tile([P, 2, 2, P], F32, name="tp")
                for a in range(2):
                    words = rows_of(2 * half + a).bitcast(F32)
                    for u in range(2):
                        nc.tensor.transpose(tp[:, a, u, :], words[:, u * P : (u + 1) * P], ident[:])
                pair.append(tp)
            banks[key] = pair

        def evacuate(key, dst):
            for half in range(2):
                nc.scalar.copy(
                    out=dst[:, 2 * half : 2 * half + 2, :, :],
                    in_=banks[key][half][:].rearrange("p a u m -> p a m u"),
                )

        def quantise(src_bf16, c_ap, s_ap):
            nc.vector.quantize_mx(out=c_ap.bitcast(FP8X4), scales=s_ap, in_=src_bf16)

        def adj_rows(g):
            ci, t0 = place[g]
            return lambda j: adj_sb[ci][:, t0 + j, :]

        def flat_bf16(t4):
            return t4[:].rearrange("p a m u -> p (a m u)").bitcast(BF16)

        def v_tiles(g):
            return 0 if g == LAST else GROUP - PE_TILES

        def degree_on_vector(g, a):
            junk_v = jpool.tile([P, 512], BF16, name="junk_v")
            nc.vector.tensor_scalar(
                out=junk_v[:],
                in0=adj_rows(g)(a),
                scalar1=1.0,
                scalar2=1.0,
                op0=ALU.mult,
                op1=ALU.add,
                accum_out=degp1[:, g, a : a + 1],
            )

        def degrees_on_tensor(g):
            first = v_tiles(g)
            d_t = dps.tile([P, GROUP - first, DEG_N], F32, name="d_t")
            sums[g] = d_t
            cols = flat_bf16(grouped[g])
            for e in range(GROUP - first):
                lo = (first + e) * 4 * P
                for t in range(4):
                    nc.tensor.matmul(
                        out=d_t[:, e, :],
                        lhsT=cols[:, lo + t : lo + 4 * P : 4],
                        rhs=ones[:, 0:DEG_N],
                        start=(t == 0),
                        stop=(t == 3),
                    )

        def add_one(g):
            nc.vector.tensor_scalar_add(
                out=degp1[:, g, v_tiles(g) : GROUP], in0=sums[g][:, :, 0], scalar1=1.0
            )

        def invert(g):
            nc.vector.reciprocal(out=recip[:, g, :], in_=degp1[:, g, :])

        def multiply(g, o_t, tiles):
            for slot, a in enumerate(tiles):
                cols = slice(a * P, (a + 1) * P)
                nc.tensor.matmul_mx(
                    out=o_t[:, slot, :],
                    lhsT=codes[g][:, cols].bitcast(FP8X4),
                    lhsT_scale=scales[g][:, cols],
                    rhs=h_codes[:].bitcast(FP8X4),
                    rhs_scale=h_scl[:],
                    start=True,
                    stop=True,
                )

        def finish(g, o_t, tiles, on_scalar):
            ci, t0 = place[g]
            n = len(tiles)
            res = rpool.tile([P, GROUP, P], F32, name="res")
            if on_scalar:
                for slot, a in enumerate(tiles):
                    nc.scalar.activation(
                        out=res[:, slot, :],
                        in_=o_t[:, slot, :],
                        func=ACT.Copy,
                        scale=recip[:, g, a : a + 1],
                    )
            else:
                nc.vector.tensor_tensor(
                    out=res[:, 0:n, :],
                    in0=o_t[:, 0:n, :],
                    in1=recip[:, g, tiles[0] : tiles[0] + n].unsqueeze(2).to_broadcast([P, n, P]),
                    op=ALU.mult,
                )
            row = t0 + tiles[0]
            nc.sync.dma_start(out=out_dst[ci][:, row : row + n, :], in_=res[:, 0:n, :])

        idle_passes(IDLE_BEFORE)
        for i in range(N_GROUPS):
            word_transposes(i, adj_rows(i))
            g_t = gpool.tile([P, GROUP, P, 2], F32, name="g_t", align_bytes=64)
            grouped[i] = g_t
            evacuate(i, g_t)
            if i == 0:
                word_transposes("x", lambda j: x_sb[:, j, :])
                evacuate("x", x_g)
                degree_on_vector(0, 0)
                nc.vector.tensor_copy(out=w_g[:], in_=w_sb[:].rearrange("p t c -> p c t"))
                quantise(w_g[:].rearrange("p c t -> p (c t)"), w_codes[:], w_scl[:])
                quantise(flat_bf16(x_g), x_codes[:], x_scl[:])
            if i == 1:
                b_ps = ops.tile([P, GROUP, P], F32, name="o_t")
                nc.tensor.matmul(out=b_ps[:, 0, :], lhsT=ones[:], rhs=bz[:], start=True, stop=True)
                nc.scalar.copy(out=bias_sb[:], in_=b_ps[:, 0, :])
                h_ps = ops.tile([P, GROUP, P], F32, name="o_t")
                for t in range(4):
                    cols = slice(t * P, (t + 1) * P)
                    nc.tensor.matmul_mx(
                        out=h_ps[:, t, :],
                        lhsT=x_codes[:, cols].bitcast(FP8X4),
                        lhsT_scale=x_scl[:, cols],
                        rhs=w_codes[:].bitcast(FP8X4),
                        rhs_scale=w_scl[:],
                        start=True,
                        stop=True,
                    )
                acc["h"] = h_ps
            if i >= 1:
                degrees_on_tensor(i - 1)
                c_t = cpool.tile([P, GROUP * P], U32, name="c_t", align_bytes=64)
                s_t = cpool.tile([P, GROUP * P], U8, name="s_t", align_bytes=64)
                codes[i - 1] = c_t
                scales[i - 1] = s_t
                quantise(flat_bf16(grouped[i - 1]), c_t[:], s_t[:])
            if i == 1:
                nc.vector.tensor_tensor(
                    out=h_g[:],
                    in0=acc["h"][:].rearrange("p t c -> p c t"),
                    in1=bias_sb[:].unsqueeze(2).to_broadcast([P, P, 4]),
                    op=ALU.add,
                )
            if i == 2:
                quantise(h_g[:].rearrange("p c t -> p (c t)"), h_codes[:], h_scl[:])
            if i >= 2:
                add_one(i - 2)
            if 1 <= i < LAST:
                degree_on_vector(i, 0)
            if i >= 2:
                invert(i - 2)
            if i >= LAG:
                o_t = ops.tile([P, GROUP, P], F32, name="o_t")
                multiply(i - LAG, o_t, range(GROUP))
                finish(i - LAG, o_t, range(GROUP), i - LAG in S_OUT)
            else:
                idle_passes(IDLE_HEAD)

        halves = (range(0, 2), range(2, GROUP))
        c_t = cpool.tile([P, GROUP * P], U32, name="c_t", align_bytes=64)
        s_t = cpool.tile([P, GROUP * P], U8, name="s_t", align_bytes=64)
        codes[LAST] = c_t
        scales[LAST] = s_t

        def quantise_half(half):
            cols = slice(2 * P * half, 2 * P * (half + 1))
            words = slice(8 * P * half, 8 * P * (half + 1))
            quantise(flat_bf16(grouped[LAST])[:, words], c_t[:, cols], s_t[:, cols])

        o_21 = ops.tile([P, GROUP, P], F32, name="o_t")
        multiply(LAST - 2, o_21, range(GROUP))
        add_one(LAST - 1)
        quantise_half(0)
        invert(LAST - 1)
        finish(LAST - 2, o_21, range(GROUP), False)
        o_22 = tps.tile([P, GROUP, P], F32, name="tp")
        multiply(LAST - 1, o_22, range(GROUP))
        finish(LAST - 1, o_22, range(GROUP), True)
        degrees_on_tensor(LAST)
        quantise_half(1)
        add_one(LAST)
        invert(LAST)
        for half in range(2):
            o_h = tps.tile([P, GROUP, P], F32, name="tp")
            multiply(LAST, o_h, halves[half])
            finish(LAST, o_h, halves[half], half == 1)
